import numpy as np
import ml_dtypes

BF16 = ml_dtypes.bfloat16


def bf(x):
    return np.asarray(x, np.float32).astype(BF16)


def f32(x):
    return np.asarray(x, np.float32)


def f64(x):
    return np.asarray(x).astype(np.float64)


def striped(idx):
    return np.tile(idx.reshape(-1, 16).T, (8, 1))


C, N, F, S = 128, 128, 128, 256


def sigmoid(v):
    return 1.0 / (1.0 + np.exp(-v))


def setup_inputs():
    return {
        "base": f32(np.random.standard_normal((C, S))),
        "x": bf(np.random.standard_normal((F, N))),
        "wa": bf(np.random.standard_normal((F, F)) / np.sqrt(F)),
        "wb": bf(np.random.standard_normal((F, F)) / np.sqrt(F)),
        "b1": f32(-3.0 + 0.5 * np.random.standard_normal((F, 1))),
        "adj": f32(np.random.uniform(0.0, 1.0, (C, N)) / 8.0),
        "offs": striped(np.random.permutation(S)[:N]),
    }


def reference(base, x, wa, wb, b1, adj, offs):
    idx = offs[:16].T.reshape(-1)
    a = f64(wa).T @ f64(x)
    b = f64(wb).T @ f64(x) + f64(b1)
    t = sigmoid(b.T[:, None, :] + a.T[None, :, :]).sum(axis=2)
    out = f64(base).copy()
    out[:, idx] = t * f64(adj)
    return out

@@ -1,0 +1,60 @@
+import concourse.mybir as mybir
+
+F32 = mybir.dt.float32
+BF16 = mybir.dt.bfloat16
+U16 = mybir.dt.uint16
+SIGMOID = mybir.ActivationFunctionType.Sigmoid
+ADD = mybir.AluOpType.add
+MULT = mybir.AluOpType.mult
+
+P = 128
+S = 256
+
+FLOPS = 2 * (2 * P * P * P) + 2 * P * P * P
+
+
+def tile_graphconvolution_gi_kernel(tc, base, x, wa, wb, b1, adj, offs, out):
+    nc = tc.nc
+    with (
+        tc.tile_pool(name="held", bufs=1) as held,
+        tc.tile_pool(name="gates", bufs=8) as gates,
+        tc.psum_pool(name="psum", bufs=1) as psum,
+    ):
+        x_sb = held.tile([P, P], BF16, name="x_sb")
+        wa_sb = held.tile([P, P], BF16, name="wa_sb")
+        wb_sb = held.tile([P, P], BF16, name="wb_sb")
+        b1_sb = held.tile([P, 1], F32, name="b1_sb")
+        adj_sb = held.tile([P, P], F32, name="adj_sb")
+        offsets = held.tile([P, P // 16], U16, name="offsets")
+        window = held.tile([P, S], F32, name="window")
+
+        nc.sync.dma_start(x_sb[:], x)
+        nc.scalar.dma_start(wb_sb[:], wb)
+        nc.sync.dma_start(wa_sb[:], wa)
+        nc.scalar.dma_start(b1_sb[:], b1)
+        nc.sync.dma_start(offsets[:], offs)
+        nc.scalar.dma_start(adj_sb[:], adj)
+        nc.sync.dma_start(window[:], base)
+
+        ones = held.tile([P, 1], BF16, name="ones")
+        nc.vector.memset(ones[:], 1.0)
+
+        b_ps = psum.tile([P, P], F32, name="b_ps")
+        a_ps = psum.tile([P, P], F32, name="a_ps")
+        nc.tensor.matmul(b_ps[:], wb_sb[:], x_sb[:], start=True, stop=True)
+        nc.tensor.matmul(a_ps[:], wa_sb[:], x_sb[:], start=True, stop=True)
+        b_sb = held.tile([P, P], F32, name="b_sb")
+        a_sb = held.tile([P, P], F32, name="a_sb")
+        nc.vector.tensor_scalar(b_sb[:], b_ps[:], b1_sb[:, 0:1], None, ADD)
+        nc.vector.tensor_copy(a_sb[:], a_ps[:])
+
+        t_ps = psum.tile([P, P], F32, name="t_ps")
+        for j in range(P):
+            gate = gates.tile([P, P], BF16, name="gate")
+            nc.scalar.activation(gate[:], b_sb[:], SIGMOID, bias=a_sb[:, j : j + 1])
+            nc.tensor.matmul(t_ps[:, j : j + 1], gate[:], ones[:], start=True, stop=True)
+
+        t_sb = held.tile([P, P], F32, name="t_sb")
+        nc.vector.tensor_copy(t_sb[:], t_ps[:])
+        nc.vector.tensor_tensor(window[:].indirect(offsets[:]), t_sb[:], adj_sb[:], MULT)
+        nc.sync.dma_start(out, window[:])

@@ -9,6 +9,7 @@ MULT = mybir.AluOpType.mult
 
 P = 128
 S = 256
+G = 8
 
 FLOPS = 2 * (2 * P * P * P) + 2 * P * P * P
 
@@ -17,7 +18,8 @@ def tile_graphconvolution_gi_kernel(tc, base, x, wa, wb, b1, adj, offs, out):
     nc = tc.nc
     with (
         tc.tile_pool(name="held", bufs=1) as held,
-        tc.tile_pool(name="gates", bufs=8) as gates,
+        tc.tile_pool(name="sums", bufs=3) as sums,
+        tc.tile_pool(name="gates", bufs=3) as gates,
         tc.psum_pool(name="psum", bufs=1) as psum,
     ):
         x_sb = held.tile([P, P], BF16, name="x_sb")
@@ -45,14 +47,24 @@ def tile_graphconvolution_gi_kernel(tc, base, x, wa, wb, b1, adj, offs, out):
         nc.tensor.matmul(a_ps[:], wa_sb[:], x_sb[:], start=True, stop=True)
         b_sb = held.tile([P, P], F32, name="b_sb")
         a_sb = held.tile([P, P], F32, name="a_sb")
-        nc.vector.tensor_scalar(b_sb[:], b_ps[:], b1_sb[:, 0:1], None, ADD)
+        nc.vector.tensor_copy(b_sb[:], b_ps[:])
         nc.vector.tensor_copy(a_sb[:], a_ps[:])
 
         t_ps = psum.tile([P, P], F32, name="t_ps")
-        for j in range(P):
-            gate = gates.tile([P, P], BF16, name="gate")
-            nc.scalar.activation(gate[:], b_sb[:], SIGMOID, bias=a_sb[:, j : j + 1])
-            nc.tensor.matmul(t_ps[:, j : j + 1], gate[:], ones[:], start=True, stop=True)
+        for group in range(P // G):
+            pair_sum = sums.tile([P, G * P], F32, name="pair_sum")
+            for i in range(G):
+                j = group * G + i
+                nc.vector.tensor_scalar(
+                    pair_sum[:, i * P : (i + 1) * P], b_sb[:], a_sb[:, j : j + 1], None, ADD
+                )
+            gate = gates.tile([P, G * P], BF16, name="gate")
+            nc.scalar.activation(gate[:], pair_sum[:], SIGMOID, bias=b1_sb[:, 0:1])
+            for i in range(G):
+                j = group * G + i
+                nc.tensor.matmul(
+                    t_ps[:, j : j + 1], gate[:, i * P : (i + 1) * P], ones[:], start=True, stop=True
+                )
 
         t_sb = held.tile([P, P], F32, name="t_sb")
         nc.vector.tensor_copy(t_sb[:], t_ps[:])

@@ -9,7 +9,8 @@ MULT = mybir.AluOpType.mult
 
 P = 128
 S = 256
-G = 8
+GROUPS = [4, 4] + [8] * 15
+assert sum(GROUPS) == P
 
 FLOPS = 2 * (2 * P * P * P) + 2 * P * P * P
 
@@ -40,6 +41,8 @@ def tile_graphconvolution_gi_kernel(tc, base, x, wa, wb, b1, adj, offs, out):
 
         ones = held.tile([P, 1], BF16, name="ones")
         nc.vector.memset(ones[:], 1.0)
+        warm = held.tile([P, 1], BF16, name="warm")
+        nc.scalar.activation(warm[:], ones[:], SIGMOID)
 
         b_ps = psum.tile([P, P], F32, name="b_ps")
         a_ps = psum.tile([P, P], F32, name="a_ps")
@@ -48,23 +51,25 @@ def tile_graphconvolution_gi_kernel(tc, base, x, wa, wb, b1, adj, offs, out):
         b_sb = held.tile([P, P], F32, name="b_sb")
         a_sb = held.tile([P, P], F32, name="a_sb")
         nc.vector.tensor_copy(b_sb[:], b_ps[:])
-        nc.vector.tensor_copy(a_sb[:], a_ps[:])
+        nc.scalar.copy(a_sb[:], a_ps[:])
 
         t_ps = psum.tile([P, P], F32, name="t_ps")
-        for group in range(P // G):
-            pair_sum = sums.tile([P, G * P], F32, name="pair_sum")
-            for i in range(G):
-                j = group * G + i
+        first = 0
+        for nodes in GROUPS:
+            pair_sum = sums.tile([P, nodes * P], F32, name="pair_sum")
+            for i in range(nodes):
+                j = first + i
                 nc.vector.tensor_scalar(
                     pair_sum[:, i * P : (i + 1) * P], b_sb[:], a_sb[:, j : j + 1], None, ADD
                 )
-            gate = gates.tile([P, G * P], BF16, name="gate")
+            gate = gates.tile([P, nodes * P], BF16, name="gate")
             nc.scalar.activation(gate[:], pair_sum[:], SIGMOID, bias=b1_sb[:, 0:1])
-            for i in range(G):
-                j = group * G + i
+            for i in range(nodes):
+                j = first + i
                 nc.tensor.matmul(
                     t_ps[:, j : j + 1], gate[:, i * P : (i + 1) * P], ones[:], start=True, stop=True
                 )
+            first += nodes
 
         t_sb = held.tile([P, P], F32, name="t_sb")
         nc.vector.tensor_copy(t_sb[:], t_ps[:])

@@ -11,6 +11,7 @@ P = 128
 S = 256
 GROUPS = [4, 4] + [8] * 15
 assert sum(GROUPS) == P
+H = 64
 
 FLOPS = 2 * (2 * P * P * P) + 2 * P * P * P
 
@@ -53,7 +54,8 @@ def tile_graphconvolution_gi_kernel(tc, base, x, wa, wb, b1, adj, offs, out):
         nc.vector.tensor_copy(b_sb[:], b_ps[:])
         nc.scalar.copy(a_sb[:], a_ps[:])
 
-        t_ps = psum.tile([P, P], F32, name="t_ps")
+        t_ps = [psum.tile([P, H], F32, name=f"t_ps{half}") for half in range(P // H)]
+        t_sb = [held.tile([P, H], F32, name=f"t_sb{half}") for half in range(P // H)]
         first = 0
         for nodes in GROUPS:
             pair_sum = sums.tile([P, nodes * P], F32, name="pair_sum")
@@ -67,11 +69,20 @@ def tile_graphconvolution_gi_kernel(tc, base, x, wa, wb, b1, adj, offs, out):
             for i in range(nodes):
                 j = first + i
                 nc.tensor.matmul(
-                    t_ps[:, j : j + 1], gate[:, i * P : (i + 1) * P], ones[:], start=True, stop=True
+                    t_ps[j // H][:, j % H : j % H + 1],
+                    gate[:, i * P : (i + 1) * P],
+                    ones[:],
+                    start=True,
+                    stop=True,
                 )
             first += nodes
-
-        t_sb = held.tile([P, P], F32, name="t_sb")
-        nc.vector.tensor_copy(t_sb[:], t_ps[:])
-        nc.vector.tensor_tensor(window[:].indirect(offsets[:]), t_sb[:], adj_sb[:], MULT)
+            if first % H == 0:
+                half = first // H - 1
+                nc.vector.tensor_copy(t_sb[half][:], t_ps[half][:])
+                nc.vector.tensor_tensor(
+                    window[:].indirect(offsets[:, half * (H // 16) : (half + 1) * (H // 16)]),
+                    t_sb[half][:],
+                    adj_sb[:, half * H : (half + 1) * H],
+                    MULT,
+                )
         nc.sync.dma_start(out, window[:])

@@ -9,7 +9,7 @@ MULT = mybir.AluOpType.mult
 
 P = 128
 S = 256
-GROUPS = [4, 4] + [8] * 15
+GROUPS = [4, 4] + [8] * 14 + [4, 2, 1, 1]
 assert sum(GROUPS) == P
 H = 64
 
@@ -20,8 +20,8 @@ def tile_graphconvolution_gi_kernel(tc, base, x, wa, wb, b1, adj, offs, out):
     nc = tc.nc
     with (
         tc.tile_pool(name="held", bufs=1) as held,
-        tc.tile_pool(name="sums", bufs=3) as sums,
-        tc.tile_pool(name="gates", bufs=3) as gates,
+        tc.tile_pool(name="sums", bufs=6) as sums,
+        tc.tile_pool(name="gates", bufs=6) as gates,
         tc.psum_pool(name="psum", bufs=1) as psum,
     ):
         x_sb = held.tile([P, P], BF16, name="x_sb")

@@ -9,8 +9,9 @@ MULT = mybir.AluOpType.mult
 
 P = 128
 S = 256
-GROUPS = [4, 4] + [8] * 14 + [4, 2, 1, 1]
-assert sum(GROUPS) == P
+DIRECT = 4
+GROUPS = [4] + [8] * 14 + [4, 2, 1, 1]
+assert DIRECT + sum(GROUPS) == P
 H = 64
 
 FLOPS = 2 * (2 * P * P * P) + 2 * P * P * P
@@ -33,8 +34,8 @@ def tile_graphconvolution_gi_kernel(tc, base, x, wa, wb, b1, adj, offs, out):
         window = held.tile([P, S], F32, name="window")
 
         nc.sync.dma_start(x_sb[:], x)
-        nc.scalar.dma_start(wb_sb[:], wb)
-        nc.sync.dma_start(wa_sb[:], wa)
+        nc.scalar.dma_start(wa_sb[:], wa)
+        nc.sync.dma_start(wb_sb[:], wb)
         nc.scalar.dma_start(b1_sb[:], b1)
         nc.sync.dma_start(offsets[:], offs)
         nc.scalar.dma_start(adj_sb[:], adj)
@@ -45,27 +46,21 @@ def tile_graphconvolution_gi_kernel(tc, base, x, wa, wb, b1, adj, offs, out):
         warm = held.tile([P, 1], BF16, name="warm")
         nc.scalar.activation(warm[:], ones[:], SIGMOID)
 
-        b_ps = psum.tile([P, P], F32, name="b_ps")
         a_ps = psum.tile([P, P], F32, name="a_ps")
-        nc.tensor.matmul(b_ps[:], wb_sb[:], x_sb[:], start=True, stop=True)
+        b_ps_scalar = psum.tile([P, P], F32, name="b_ps_scalar")
+        b_ps_vector = psum.tile([P, P], F32, name="b_ps_vector")
         nc.tensor.matmul(a_ps[:], wa_sb[:], x_sb[:], start=True, stop=True)
+        nc.tensor.matmul(b_ps_scalar[:], wb_sb[:], x_sb[:], start=True, stop=True)
+        nc.tensor.matmul(b_ps_vector[:], wb_sb[:], x_sb[:], start=True, stop=True)
+        ab1_sb = held.tile([P, P], F32, name="ab1_sb")
         b_sb = held.tile([P, P], F32, name="b_sb")
-        a_sb = held.tile([P, P], F32, name="a_sb")
-        nc.vector.tensor_copy(b_sb[:], b_ps[:])
-        nc.scalar.copy(a_sb[:], a_ps[:])
+        nc.vector.tensor_scalar(ab1_sb[:], a_ps[:], b1_sb[:, 0:1], None, ADD)
+        nc.vector.tensor_copy(b_sb[:], b_ps_vector[:])
 
         t_ps = [psum.tile([P, H], F32, name=f"t_ps{half}") for half in range(P // H)]
         t_sb = [held.tile([P, H], F32, name=f"t_sb{half}") for half in range(P // H)]
-        first = 0
-        for nodes in GROUPS:
-            pair_sum = sums.tile([P, nodes * P], F32, name="pair_sum")
-            for i in range(nodes):
-                j = first + i
-                nc.vector.tensor_scalar(
-                    pair_sum[:, i * P : (i + 1) * P], b_sb[:], a_sb[:, j : j + 1], None, ADD
-                )
-            gate = gates.tile([P, nodes * P], BF16, name="gate")
-            nc.scalar.activation(gate[:], pair_sum[:], SIGMOID, bias=b1_sb[:, 0:1])
+
+        def sum_over_features(gate, first, nodes):
             for i in range(nodes):
                 j = first + i
                 nc.tensor.matmul(
@@ -75,6 +70,25 @@ def tile_graphconvolution_gi_kernel(tc, base, x, wa, wb, b1, adj, offs, out):
                     start=True,
                     stop=True,
                 )
+
+        gate = gates.tile([P, DIRECT * P], BF16, name="gate")
+        for j in range(DIRECT):
+            nc.scalar.activation(
+                gate[:, j * P : (j + 1) * P], b_ps_scalar[:], SIGMOID, bias=ab1_sb[:, j : j + 1]
+            )
+        sum_over_features(gate, 0, DIRECT)
+
+        first = DIRECT
+        for nodes in GROUPS:
+            pair_sum = sums.tile([P, nodes * P], F32, name="pair_sum")
+            for i in range(nodes):
+                j = first + i
+                nc.vector.tensor_scalar(
+                    pair_sum[:, i * P : (i + 1) * P], b_sb[:], ab1_sb[:, j : j + 1], None, ADD
+                )
+            gate = gates.tile([P, nodes * P], BF16, name="gate")
+            nc.scalar.activation(gate[:], pair_sum[:], SIGMOID)
+            sum_over_features(gate, first, nodes)
             first += nodes
             if first % H == 0:
                 half = first // H - 1

@@ -10,7 +10,7 @@ MULT = mybir.AluOpType.mult
 P = 128
 S = 256
 DIRECT = 4
-GROUPS = [4] + [8] * 14 + [4, 2, 1, 1]
+GROUPS = [4, 4, 4] + [8] * 13 + [4, 2, 1, 1]
 assert DIRECT + sum(GROUPS) == P
 H = 64
 
@@ -34,8 +34,8 @@ def tile_graphconvolution_gi_kernel(tc, base, x, wa, wb, b1, adj, offs, out):
         window = held.tile([P, S], F32, name="window")
 
         nc.sync.dma_start(x_sb[:], x)
-        nc.scalar.dma_start(wa_sb[:], wa)
-        nc.sync.dma_start(wb_sb[:], wb)
+        nc.scalar.dma_start(wb_sb[:], wb)
+        nc.sync.dma_start(wa_sb[:], wa)
         nc.scalar.dma_start(b1_sb[:], b1)
         nc.sync.dma_start(offsets[:], offs)
         nc.scalar.dma_start(adj_sb[:], adj)
@@ -49,13 +49,14 @@ def tile_graphconvolution_gi_kernel(tc, base, x, wa, wb, b1, adj, offs, out):
         a_ps = psum.tile([P, P], F32, name="a_ps")
         b_ps_scalar = psum.tile([P, P], F32, name="b_ps_scalar")
         b_ps_vector = psum.tile([P, P], F32, name="b_ps_vector")
-        nc.tensor.matmul(a_ps[:], wa_sb[:], x_sb[:], start=True, stop=True)
-        nc.tensor.matmul(b_ps_scalar[:], wb_sb[:], x_sb[:], start=True, stop=True)
         nc.tensor.matmul(b_ps_vector[:], wb_sb[:], x_sb[:], start=True, stop=True)
+        nc.tensor.matmul(b_ps_scalar[:], wb_sb[:], x_sb[:], start=True, stop=True)
+        nc.tensor.matmul(a_ps[:], wa_sb[:], x_sb[:], start=True, stop=True)
         ab1_sb = held.tile([P, P], F32, name="ab1_sb")
         b_sb = held.tile([P, P], F32, name="b_sb")
-        nc.vector.tensor_scalar(ab1_sb[:], a_ps[:], b1_sb[:, 0:1], None, ADD)
+        early = DIRECT + GROUPS[0]
         nc.vector.tensor_copy(b_sb[:], b_ps_vector[:])
+        nc.vector.tensor_scalar(ab1_sb[:, 0:early], a_ps[:, 0:early], b1_sb[:, 0:1], None, ADD)
 
         t_ps = [psum.tile([P, H], F32, name=f"t_ps{half}") for half in range(P // H)]
         t_sb = [held.tile([P, H], F32, name=f"t_sb{half}") for half in range(P // H)]
@@ -85,6 +86,10 @@ def tile_graphconvolution_gi_kernel(tc, base, x, wa, wb, b1, adj, offs, out):
                 j = first + i
                 nc.vector.tensor_scalar(
                     pair_sum[:, i * P : (i + 1) * P], b_sb[:], ab1_sb[:, j : j + 1], None, ADD
+                )
+            if first == DIRECT:
+                nc.vector.tensor_scalar(
+                    ab1_sb[:, early:P], a_ps[:, early:P], b1_sb[:, 0:1], None, ADD
                 )
             gate = gates.tile([P, nodes * P], BF16, name="gate")
             nc.scalar.activation(gate[:], pair_sum[:], SIGMOID)

@@ -47,15 +47,13 @@ def tile_graphconvolution_gi_kernel(tc, base, x, wa, wb, b1, adj, offs, out):
         nc.scalar.activation(warm[:], ones[:], SIGMOID)
 
         a_ps = psum.tile([P, P], F32, name="a_ps")
-        b_ps_scalar = psum.tile([P, P], F32, name="b_ps_scalar")
-        b_ps_vector = psum.tile([P, P], F32, name="b_ps_vector")
-        nc.tensor.matmul(b_ps_vector[:], wb_sb[:], x_sb[:], start=True, stop=True)
-        nc.tensor.matmul(b_ps_scalar[:], wb_sb[:], x_sb[:], start=True, stop=True)
+        b_ps = psum.tile([P, P], F32, name="b_ps")
+        nc.tensor.matmul(b_ps[:], wb_sb[:], x_sb[:], start=True, stop=True)
         nc.tensor.matmul(a_ps[:], wa_sb[:], x_sb[:], start=True, stop=True)
         ab1_sb = held.tile([P, P], F32, name="ab1_sb")
         b_sb = held.tile([P, P], F32, name="b_sb")
         early = DIRECT + GROUPS[0]
-        nc.vector.tensor_copy(b_sb[:], b_ps_vector[:])
+        nc.vector.tensor_copy(b_sb[:], b_ps[:])
         nc.vector.tensor_scalar(ab1_sb[:, 0:early], a_ps[:, 0:early], b1_sb[:, 0:1], None, ADD)
 
         t_ps = [psum.tile([P, H], F32, name=f"t_ps{half}") for half in range(P // H)]
@@ -75,7 +73,7 @@ def tile_graphconvolution_gi_kernel(tc, base, x, wa, wb, b1, adj, offs, out):
         gate = gates.tile([P, DIRECT * P], BF16, name="gate")
         for j in range(DIRECT):
             nc.scalar.activation(
-                gate[:, j * P : (j + 1) * P], b_ps_scalar[:], SIGMOID, bias=ab1_sb[:, j : j + 1]
+                gate[:, j * P : (j + 1) * P], b_sb[:], SIGMOID, bias=ab1_sb[:, j : j + 1]
             )
         sum_over_features(gate, 0, DIRECT)
 

@@ -10,7 +10,7 @@ MULT = mybir.AluOpType.mult
 P = 128
 S = 256
 DIRECT = 4
-GROUPS = [4, 4, 4] + [8] * 13 + [4, 2, 1, 1]
+GROUPS = [4, 4, 4, 8, 8, 16, 16] + [16, 16, 16, 8, 4, 2, 1, 1]
 assert DIRECT + sum(GROUPS) == P
 H = 64
 

@@ -38,7 +38,7 @@ def tile_graphconvolution_gi_kernel(tc, base, x, wa, wb, b1, adj, offs, out):
         nc.sync.dma_start(wa_sb[:], wa)
         nc.scalar.dma_start(b1_sb[:], b1)
         nc.sync.dma_start(offsets[:], offs)
-        nc.scalar.dma_start(adj_sb[:], adj)
+        nc.sync.dma_start(adj_sb[:], adj)
         nc.sync.dma_start(window[:], base)
 
         ones = held.tile([P, 1], BF16, name="ones")

@@ -46,15 +46,17 @@ def tile_graphconvolution_gi_kernel(tc, base, x, wa, wb, b1, adj, offs, out):
         warm = held.tile([P, 1], BF16, name="warm")
         nc.scalar.activation(warm[:], ones[:], SIGMOID)
 
-        a_ps = psum.tile([P, P], F32, name="a_ps")
+        early = DIRECT + GROUPS[0]
         b_ps = psum.tile([P, P], F32, name="b_ps")
+        a_early_ps = psum.tile([P, early], F32, name="a_early_ps")
+        a_late_ps = psum.tile([P, P - early], F32, name="a_late_ps")
         nc.tensor.matmul(b_ps[:], wb_sb[:], x_sb[:], start=True, stop=True)
-        nc.tensor.matmul(a_ps[:], wa_sb[:], x_sb[:], start=True, stop=True)
+        nc.tensor.matmul(a_early_ps[:], wa_sb[:], x_sb[:, 0:early], start=True, stop=True)
+        nc.tensor.matmul(a_late_ps[:], wa_sb[:], x_sb[:, early:P], start=True, stop=True)
         ab1_sb = held.tile([P, P], F32, name="ab1_sb")
         b_sb = held.tile([P, P], F32, name="b_sb")
-        early = DIRECT + GROUPS[0]
         nc.vector.tensor_copy(b_sb[:], b_ps[:])
-        nc.vector.tensor_scalar(ab1_sb[:, 0:early], a_ps[:, 0:early], b1_sb[:, 0:1], None, ADD)
+        nc.vector.tensor_scalar(ab1_sb[:, 0:early], a_early_ps[:], b1_sb[:, 0:1], None, ADD)
 
         t_ps = [psum.tile([P, H], F32, name=f"t_ps{half}") for half in range(P // H)]
         t_sb = [held.tile([P, H], F32, name=f"t_sb{half}") for half in range(P // H)]
@@ -87,7 +89,7 @@ def tile_graphconvolution_gi_kernel(tc, base, x, wa, wb, b1, adj, offs, out):
                 )
             if first == DIRECT:
                 nc.vector.tensor_scalar(
-                    ab1_sb[:, early:P], a_ps[:, early:P], b1_sb[:, 0:1], None, ADD
+                    ab1_sb[:, early:P], a_late_ps[:], b1_sb[:, 0:1], None, ADD
                 )
             gate = gates.tile([P, nodes * P], BF16, name="gate")
             nc.scalar.activation(gate[:], pair_sum[:], SIGMOID)

import concourse.mybir as mybir

F32 = mybir.dt.float32
BF16 = mybir.dt.bfloat16
U16 = mybir.dt.uint16
SIGMOID = mybir.ActivationFunctionType.Sigmoid
ADD = mybir.AluOpType.add
MULT = mybir.AluOpType.mult

P = 128
S = 256
DIRECT = 4
GROUPS = [4, 4, 4, 8, 8, 16, 16] + [16, 16, 16, 8, 4, 2, 1, 1]
assert DIRECT + sum(GROUPS) == P
H = 64

FLOPS = 2 * (2 * P * P * P) + 2 * P * P * P


def tile_graphconvolution_gi_kernel(tc, base, x, wa, wb, b1, adj, offs, out):
    nc = tc.nc
    with (
        tc.tile_pool(name="held", bufs=1) as held,
        tc.tile_pool(name="sums", bufs=6) as sums,
        tc.tile_pool(name="gates", bufs=6) as gates,
        tc.psum_pool(name="psum", bufs=1) as psum,
    ):
        x_sb = held.tile([P, P], BF16, name="x_sb")
        wa_sb = held.tile([P, P], BF16, name="wa_sb")
        wb_sb = held.tile([P, P], BF16, name="wb_sb")
        b1_sb = held.tile([P, 1], F32, name="b1_sb")
        adj_sb = held.tile([P, P], F32, name="adj_sb")
        offsets = held.tile([P, P // 16], U16, name="offsets")
        window = held.tile([P, S], F32, name="window")

        nc.sync.dma_start(x_sb[:], x)
        nc.scalar.dma_start(wb_sb[:], wb)
        nc.sync.dma_start(wa_sb[:], wa)
        nc.scalar.dma_start(b1_sb[:], b1)
        nc.sync.dma_start(offsets[:], offs)
        nc.sync.dma_start(adj_sb[:], adj)
        nc.sync.dma_start(window[:], base)

        ones = held.tile([P, 1], BF16, name="ones")
        nc.vector.memset(ones[:], 1.0)
        warm = held.tile([P, 1], BF16, name="warm")
        nc.scalar.activation(warm[:], ones[:], SIGMOID)

        early = DIRECT + GROUPS[0]
        b_ps = psum.tile([P, P], F32, name="b_ps")
        a_early_ps = psum.tile([P, early], F32, name="a_early_ps")
        a_late_ps = psum.tile([P, P - early], F32, name="a_late_ps")
        nc.tensor.matmul(b_ps[:], wb_sb[:], x_sb[:], start=True, stop=True)
        nc.tensor.matmul(a_early_ps[:], wa_sb[:], x_sb[:, 0:early], start=True, stop=True)
        nc.tensor.matmul(a_late_ps[:], wa_sb[:], x_sb[:, early:P], start=True, stop=True)
        ab1_sb = held.tile([P, P], F32, name="ab1_sb")
        b_sb = held.tile([P, P], F32, name="b_sb")
        nc.vector.tensor_copy(b_sb[:], b_ps[:])
        nc.vector.tensor_scalar(ab1_sb[:, 0:early], a_early_ps[:], b1_sb[:, 0:1], None, ADD)

        t_ps = [psum.tile([P, H], F32, name=f"t_ps{half}") for half in range(P // H)]
        t_sb = [held.tile([P, H], F32, name=f"t_sb{half}") for half in range(P // H)]

        def sum_over_features(gate, first, nodes):
            for i in range(nodes):
                j = first + i
                nc.tensor.matmul(
                    t_ps[j // H][:, j % H : j % H + 1],
                    gate[:, i * P : (i + 1) * P],
                    ones[:],
                    start=True,
                    stop=True,
                )

        gate = gates.tile([P, DIRECT * P], BF16, name="gate")
        for j in range(DIRECT):
            nc.scalar.activation(
                gate[:, j * P : (j + 1) * P], b_sb[:], SIGMOID, bias=ab1_sb[:, j : j + 1]
            )
        sum_over_features(gate, 0, DIRECT)

        first = DIRECT
        for nodes in GROUPS:
            pair_sum = sums.tile([P, nodes * P], F32, name="pair_sum")
            for i in range(nodes):
                j = first + i
                nc.vector.tensor_scalar(
                    pair_sum[:, i * P : (i + 1) * P], b_sb[:], ab1_sb[:, j : j + 1], None, ADD
                )
            if first == DIRECT:
                nc.vector.tensor_scalar(
                    ab1_sb[:, early:P], a_late_ps[:], b1_sb[:, 0:1], None, ADD
                )
            gate = gates.tile([P, nodes * P], BF16, name="gate")
            nc.scalar.activation(gate[:], pair_sum[:], SIGMOID)
            sum_over_features(gate, first, nodes)
            first += nodes
            if first % H == 0:
                half = first // H - 1
                nc.vector.tensor_copy(t_sb[half][:], t_ps[half][:])
                nc.vector.tensor_tensor(
                    window[:].indirect(offsets[:, half * (H // 16) : (half + 1) * (H // 16)]),
                    t_sb[half][:],
                    adj_sb[:, half * H : (half + 1) * H],
                    MULT,
                )
        nc.sync.dma_start(out, window[:])
